import numpy as np
import ml_dtypes


def mxq(x, axis, fmt="e4m3"):
    dtype, down = {"e4m3": (ml_dtypes.float8_e4m3fn, 7), "e5m2": (ml_dtypes.float8_e5m2, 14)}[fmt]
    v = np.moveaxis(np.asarray(x, np.float32).astype(ml_dtypes.bfloat16).astype(np.float64), axis, -1)
    blocks = v.reshape(v.shape[:-1] + (-1, 32))
    amax = np.abs(blocks).max(-1, keepdims=True)
    byte = np.maximum(np.where(amax > 0, np.frexp(amax)[1] - 1 + 127, 0) - down, 1)
    scale = np.exp2(byte - 127.0)
    codes = (blocks / scale).astype(np.float32).astype(dtype).astype(np.float64)
    return np.moveaxis((codes * scale).reshape(v.shape), -1, axis)


WIDE = False


def mx_kscale(k):
    if not WIDE:
        return np.ones(k)
    levels = np.array([10, -10, 5, -5, 0])
    if k % 512:
        return np.exp2(np.random.permutation(np.resize(levels, k // 32))).repeat(32)
    a = np.empty((k // 512, 16))
    for p in range(k // 512):
        a[p, :8] = np.random.permutation(np.resize(levels, 8))
        for g in range(8):
            far = levels[np.abs(levels - a[p, g]) >= 10]
            a[p, g + 8] = far[np.random.randint(len(far))]
    return np.exp2(a.ravel()).repeat(32)


BF16 = ml_dtypes.bfloat16


def bf(x):
    return np.asarray(x, np.float32).astype(BF16)


def f64(x):
    return np.asarray(x).astype(np.float64)


E2M1 = np.array([0.0, 0.5, 1.0, 1.5, 2.0, 3.0, 4.0, 6.0, -0.0, -0.5, -1.0, -1.5, -2.0, -3.0, -4.0, -6.0])


def pack_weight(w, fmt):
    k, n = w.shape
    w = f64(bf(w)).reshape(k // 32, 32, n)
    amax = np.abs(w).max(1)
    if fmt == "e4m3":
        byte = np.frexp(amax)[1] - 1 + 127 - 7
    else:
        mant, ex = np.frexp(amax / 6.0)
        byte = np.where(mant > 0.5, ex, ex - 1) + 127
    byte = np.clip(np.where(amax > 0, byte, 1), 1, 254)
    scaled = (w * np.exp2(127.0 - byte)[:, None, :]).reshape(k, n).astype(np.float32)
    by_word = np.ascontiguousarray(scaled.reshape(k // 512, 128, 4, n).transpose(0, 1, 3, 2))
    if fmt == "e4m3":
        words = by_word.astype(ml_dtypes.float8_e4m3fn).view(np.uint8)
    else:
        c = by_word.astype(ml_dtypes.float4_e2m1fn).view(np.uint8) & 0xF
        words = c[..., 0::2] | (c[..., 1::2] << 4)
    return np.ascontiguousarray(words), np.ascontiguousarray(byte.astype(np.uint8).reshape(k // 512, 16, n))


def unpack_weight(words, scales, fmt):
    g, p, n, _ = words.shape
    if fmt == "e4m3":
        vals = np.ascontiguousarray(words).view(ml_dtypes.float8_e4m3fn).astype(np.float64)
    else:
        nib = np.empty((g, p, n, 4), np.uint8)
        nib[..., 0::2] = words & 0xF
        nib[..., 1::2] = words >> 4
        vals = E2M1[nib]
    vals = vals * np.repeat(np.exp2(scales.astype(np.float64) - 127.0), 8, axis=1)[..., None]
    return vals.transpose(0, 1, 3, 2).reshape(g * 512, n)
def pack4(w):
    words, scales = pack_weight(w, "e2m1")
    return words.reshape(words.shape[0], 128, -1), scales


def unpack4(words, scales):
    return unpack_weight(words.reshape(words.shape[0], 128, -1, 2), scales, "e2m1")


B, C, H, W = 8, 512, 16, 32
N = H * W
SIG = 3.0


def draw0():
    s, t = mx_kscale(C), mx_kscale(C)
    r = np.sqrt(SIG / np.sqrt(C))
    q_ir = bf(np.random.standard_normal((B, C, N)) * r / t[:, None])
    irSegF = bf(np.random.standard_normal((B, C, H, W)) * s[:, None, None])
    wk = np.random.standard_normal((C, C)) * r / np.sqrt(C) * t[:, None] / s[None, :]
    words, scales = pack4(np.ascontiguousarray(wk.T))
    return {
        "q_ir": q_ir,
        "irSegF": irSegF,
        "Wk_dr_words": words,
        "Wk_dr_scales": scales,
        "bk_dr": bf(np.random.standard_normal(C) * 0.1 * t),
    }


def core(q_ir, irSegF, Wk_dr_words, Wk_dr_scales, bk_dr):
    seg = f64(irSegF).reshape(B, C, N)
    key = (unpack4(Wk_dr_words, Wk_dr_scales).T @ mxq(seg, 1, "e4m3")) + f64(bk_dr)[None, :, None]
    s = mxq(f64(q_ir), 1, "e4m3").transpose(0, 2, 1) @ mxq(key, 1, "e4m3")
    e = np.exp(s - s.max(1, keepdims=True))
    return e / e.sum(1, keepdims=True)


def e4m3fn_bytes(y):
    return np.clip(np.asarray(y, np.float64), -448.0, 448.0).astype(np.float32).astype(ml_dtypes.float8_e4m3fn).view(np.uint8)


def e4m3fn_values(b):
    return np.asarray(b, np.uint8).view(ml_dtypes.float8_e4m3fn).astype(np.float64)


def setup_inputs():
    d = draw0()
    x0 = np.asarray(d['q_ir']).astype(np.float64)
    s = (np.max(np.abs(x0), axis=(0, 2), keepdims=True) / 448.0).astype(np.float32)
    out = {}
    for k, v in d.items():
        if k == 'q_ir':
            out['q_ir_bytes'] = e4m3fn_bytes(x0 / s.astype(np.float64))
            out['q_ir_scale'] = s
        else:
            out[k] = v
    return out


def reference(q_ir_bytes, q_ir_scale, irSegF, Wk_dr_words, Wk_dr_scales, bk_dr):
    return core(e4m3fn_values(q_ir_bytes) * q_ir_scale.astype(np.float64), irSegF, Wk_dr_words, Wk_dr_scales, bk_dr)

@@ -1,0 +1,333 @@
+from contextlib import ExitStack
+
+import concourse.mybir as mybir
+from concourse.masks import make_identity
+
+F32 = mybir.dt.float32
+BF16 = mybir.dt.bfloat16
+I32 = mybir.dt.int32
+U32 = mybir.dt.uint32
+U8 = mybir.dt.uint8
+FP8 = mybir.dt.float8_e4m3fn
+FP8X4 = mybir.dt.float8_e4m3fn_x4
+FP4X4 = mybir.dt.float4_e2m1fn_x4
+ACT = mybir.ActivationFunctionType
+ALU = mybir.AluOpType
+AX = mybir.AxisListType
+
+B = 8
+C = 512
+N = 512
+P = 128
+PACK = 4
+SEGI_BUFS = 3
+SEG_ENG = "gggs"
+NORM_ENG = "gggg"
+FLOPS = 2 * B * C * C * N * 2
+
+
+def tile_featuremaptransformer_pb_t_w4_kernel(tc, q_bytes, q_scale, seg, w_words, w_scales, bias, out):
+    nc = tc.nc
+    seg_v = seg.rearrange("b (p t) h w -> b p t (h w)", t=PACK)
+    q_v = q_bytes.rearrange("b (p t) n -> b p (t n)", t=PACK)
+
+    with ExitStack() as ctx:
+        keep = ctx.enter_context(tc.tile_pool(name="keep", bufs=1))
+        work = ctx.enter_context(tc.tile_pool(name="work", bufs=2))
+        psum = ctx.enter_context(tc.psum_pool(name="psum", bufs=1))
+
+        w_raw = keep.tile([P, 2 * C], U8, name="w_raw", align_bytes=64)
+        w_cod = keep.tile([P, 2 * C], U8, name="w_cod", align_bytes=64)
+        s_raw = keep.tile([P, C], U8, name="s_raw", align_bytes=64)
+        w_scl = keep.tile([P, C], U8, name="w_scl", align_bytes=64)
+        bias_b = keep.tile([P, PACK], BF16, name="bias_b")
+        bias_f = keep.tile([P, PACK], F32, name="bias_f")
+        qs = keep.tile([P, PACK], F32, name="qs")
+        ident = keep.tile([P, P], F32, name="ident")
+        dummy = keep.tile([P, 1], F32, name="dummy")
+        seg_raw = [keep.tile([P, PACK, N], BF16, name="seg_raw%d" % b, align_bytes=64) for b in range(B)]
+        q_raw = [keep.tile([P, PACK * N], U8, name="q_raw%d" % b, align_bytes=64) for b in range(B)]
+
+        T = {}
+
+        def load_seg(b, m0, m1):
+            nc.sync.dma_start(out=seg_raw[b][:, :, m0:m1], in_=seg_v[b][:, :, m0:m1])
+
+        def load_q(b):
+            nc.sync.dma_start(out=q_raw[b][:], in_=q_v[b])
+
+        def new(key, b, shape, dt, bufs=2):
+            t = work.tile(shape, dt, name=key, tag=key, bufs=bufs, align_bytes=64)
+            T[key, b] = t
+            return t
+
+        def seg_group(b, m0, m1, eng):
+            t = T["segi", b]
+            dst = t[:, m0:m1, :].rearrange("p (c i) t -> p c t i", i=4)
+            src = seg_raw[b][:, :, m0:m1].rearrange("p t (c i) -> p c t i", i=4)
+            if eng == "v":
+                nc.vector.tensor_copy(out=dst, in_=src)
+            elif eng == "s":
+                nc.scalar.copy(dst, src)
+            else:
+                nc.gpsimd.tensor_scalar(dst, src, 1.0, 0.0, op0=ALU.mult, op1=ALU.add)
+
+        def segint(b, eng, parts=4):
+            new("segi", b, [P, N, PACK], BF16, bufs=SEGI_BUFS)
+            w = N // parts
+            for k in range(parts):
+                seg_group(b, k * w, (k + 1) * w, eng[k % len(eng)])
+
+        def q1_part(b, m0, m1):
+            nc.vector.quantize_mx(
+                out=T["segc", b][:, m0:m1].bitcast(FP8X4),
+                scales=T["segs", b][:, m0:m1],
+                in_=T["segi", b][:, m0:m1, :].rearrange("p n t -> p (n t)"),
+            )
+
+        def q1(b):
+            new("segc", b, [P, N], U32)
+            new("segs", b, [P, N], U8)
+            q1_part(b, 0, N)
+
+        def m1(b, j):
+            bank = psum.tile([P, PACK, P], F32, name="bank", tag="bank", bufs=6)
+            T["kb", b, j] = bank
+            for t in range(PACK):
+                nc.tensor.matmul_mx(
+                    out=bank[:, t, :],
+                    lhsT=w_cod[:, 2 * P * t : 2 * P * (t + 1)].bitcast(FP4X4),
+                    lhsT_scale=w_scl[:, P * t : P * (t + 1)],
+                    rhs=T["segc", b][:, P * j : P * (j + 1)].bitcast(FP8X4),
+                    rhs_scale=T["segs", b][:, P * j : P * (j + 1)],
+                    start=True,
+                    stop=True,
+                )
+
+        def ke(b, j):
+            if j == 0:
+                new("keyi", b, [P, N, PACK], BF16)
+            nc.vector.tensor_tensor(
+                out=T["keyi", b][:, P * j : P * (j + 1), :],
+                in0=T["kb", b, j][:].rearrange("p t n -> p n t"),
+                in1=bias_f[:].unsqueeze(1).to_broadcast([P, P, PACK]),
+                op=ALU.add,
+            )
+
+        def quant(src, cod, scl, b):
+            c = new(cod, b, [P, N], U32)
+            s = new(scl, b, [P, N], U8)
+            nc.vector.quantize_mx(
+                out=c[:].bitcast(FP8X4), scales=s[:], in_=T[src, b][:].rearrange("p n t -> p (n t)")
+            )
+
+        def widen(b):
+            w = new("qw", b, [P, PACK, N], BF16, bufs=3)
+            for t in range(PACK):
+                nc.scalar.activation(
+                    out=w[:, t, :],
+                    in_=q_raw[b][:, N * t : N * (t + 1)].bitcast(FP8),
+                    func=ACT.Copy,
+                    scale=qs[:, t : t + 1],
+                )
+
+        def qint(b, engs="v"):
+            d = new("qi", b, [P, N, PACK], BF16)
+            w = N // len(engs)
+            for k, e in enumerate(engs):
+                dst = d[:, k * w : (k + 1) * w, :].rearrange("p (c i) t -> p c t i", i=4)
+                src = T["qw", b][:, :, k * w : (k + 1) * w].rearrange("p t (c i) -> p c t i", i=4)
+                if e == "v":
+                    nc.vector.tensor_copy(out=dst, in_=src)
+                elif e == "s":
+                    nc.scalar.copy(dst, src)
+                else:
+                    nc.gpsimd.tensor_scalar(dst, src, 1.0, 0.0, op0=ALU.mult, op1=ALU.add)
+
+        def m2(b, mt):
+            bank = psum.tile([P, N], F32, name="bank", tag="bank", bufs=6)
+            T["sb", b, mt] = bank
+            nc.tensor.matmul_mx(
+                out=bank[:],
+                lhsT=T["keyc", b][:, P * mt : P * (mt + 1)].bitcast(FP8X4),
+                lhsT_scale=T["keys", b][:, P * mt : P * (mt + 1)],
+                rhs=T["qc", b][:].bitcast(FP8X4),
+                rhs_scale=T["qsc", b][:],
+                start=True,
+                stop=True,
+            )
+
+        def xmax(b, mt):
+            if mt == 0:
+                new("nmax", b, [P, 4], F32, bufs=3)
+            nc.vector.tensor_reduce(
+                out=T["nmax", b][:, mt : mt + 1], in_=T["sb", b, mt][:], axis=AX.X, op=ALU.max, negate=True
+            )
+
+        def expo(b, mt):
+            if mt == 0:
+                new("sum", b, [P, 4], F32, bufs=3)
+                new("e", b, [P, 4, N], F32, bufs=3)
+            nc.scalar.activation(
+                out=T["e", b][:, mt, :],
+                in_=T["sb", b, mt][:],
+                func=ACT.Exp,
+                bias=T["nmax", b][:, mt : mt + 1],
+                accum_out=T["sum", b][:, mt : mt + 1],
+            )
+
+        def recip(b, m0=0, m1=4):
+            if m0 == 0:
+                new("r", b, [P, 4], F32, bufs=3)
+            nc.vector.reciprocal(out=T["r", b][:, m0:m1], in_=T["sum", b][:, m0:m1])
+
+        def norm(b, mt, eng):
+            e = T["e", b][:, mt, :]
+            r = T["r", b][:, mt : mt + 1]
+            if eng == "v":
+                nc.vector.tensor_scalar(e, e, r, None, op0=ALU.mult)
+            elif eng == "s":
+                nc.scalar.activation(out=e, in_=e, func=ACT.Copy, scale=r)
+            else:
+                nc.gpsimd.tensor_scalar(e, e, r, 0.0, op0=ALU.mult, op1=ALU.add)
+
+        def trans(b, c):
+            if b == B - 2:
+                bank = psum.tile([P, 4, P], F32, name="bank", tag="bank", bufs=6)
+            else:
+                bank = psum.tile([P, 4, P], F32, name="tbank", tag="tbank", bufs=2)
+            T["tb", b, c] = bank
+            for mt in range(4):
+                nc.tensor.transpose(bank[:, mt, :], T["e", b][:, mt, P * c : P * (c + 1)], ident[:])
+
+        def tail_store(b, mt, eng):
+            bank = psum.tile([P, 4, P], F32, name="bank", tag="bank", bufs=6)
+            for c in range(4):
+                nc.tensor.transpose(bank[:, c, :], T["e", b][:, mt, P * c : P * (c + 1)], ident[:])
+            o = work.tile([P, 4, P], F32, name="o", tag="o", bufs=8)
+            dst = out[b].rearrange("(c p) m -> p c m", p=P)
+            for k, e in enumerate(eng):
+                w = 4 // len(eng)
+                cs = slice(k * w, (k + 1) * w)
+                if e == "s":
+                    nc.scalar.copy(o[:, cs, :], bank[:, cs, :])
+                else:
+                    nc.vector.tensor_copy(out=o[:, cs, :], in_=bank[:, cs, :])
+                nc.sync.dma_start(out=dst[:, cs, P * mt : P * (mt + 1)], in_=o[:, cs, :])
+
+        def evac(b, c, eng):
+            o = work.tile([P, N], F32, name="o", tag="o", bufs=8)
+            src = T["tb", b, c][:].rearrange("p t m -> p (t m)")
+            if eng == "s":
+                nc.scalar.copy(o[:], src)
+            else:
+                nc.vector.tensor_copy(out=o[:], in_=src)
+            nc.sync.dma_start(out=out[b, P * c : P * (c + 1), :], in_=o[:])
+
+        with tc.manual_schedule():
+            nc.vector.memset(s_raw[:].bitcast(I32), 0)
+            nc.vector.memset(dummy[:], 0.0)
+            nc.gpsimd.dma_start(out=qs[:], in_=q_scale.rearrange("o (p t) u -> p (o t u)", t=PACK))
+            nc.gpsimd.dma_start(out=bias_b[:], in_=bias.rearrange("(p t) -> p t", t=PACK))
+            load_seg(0, 0, N // 2)
+            nc.sync.dma_start(out=w_raw[:], in_=w_words[0])
+            for quad in range(4):
+                nc.sync.dma_start(
+                    out=s_raw[32 * quad : 32 * quad + 4, :].bitcast(I32),
+                    in_=w_scales[0, 4 * quad : 4 * quad + 4, :].bitcast(I32),
+                )
+            load_seg(0, N // 2, N)
+            load_q(0)
+            for b in range(1, B):
+                load_seg(b, 0, N)
+                load_q(b)
+            nc.scalar.activation(out=dummy[:], in_=dummy[:], func=ACT.Exp)
+            make_identity(nc, ident[:])
+
+            new("segi", 0, [P, N, PACK], BF16, bufs=SEGI_BUFS)
+            new("segc", 0, [P, N], U32)
+            new("segs", 0, [P, N], U8)
+            seg_group(0, 0, N // 2, "v")
+            nc.vector.tensor_copy(
+                out=w_cod[:].rearrange("p (t m e) -> p t m e", t=4, e=2),
+                in_=w_raw[:].rearrange("p (m t e) -> p t m e", t=4, e=2),
+            )
+            nc.vector.tensor_copy(
+                out=w_scl[:].rearrange("p (t m) -> p t m", t=4), in_=s_raw[:].rearrange("p (m t) -> p t m", t=4)
+            )
+            q1_part(0, 0, N // 2)
+            seg_group(0, N // 2, N, "v")
+            m1(0, 0)
+            m1(0, 1)
+            q1_part(0, N // 2, N)
+            m1(0, 2)
+            m1(0, 3)
+            nc.scalar.copy(bias_f[:], bias_b[:])
+            widen(0)
+            segint(1, "gggs")
+            for j in range(4):
+                ke(0, j)
+            qint(0, "v")
+            widen(1)
+            segint(2, SEG_ENG)
+            widen(2)
+            quant("qi", "qc", "qsc", 0)
+
+            for b in range(1, B):
+                q1(b)
+                for j in range(4):
+                    m1(b, j)
+                qint(b, "v")
+                if b >= B - 0:
+                    recip(b - 2)
+                    for mt in range(4):
+                        norm(b - 2, mt, "ssss"[mt])
+                quant("keyi", "keyc", "keys", b - 1)
+                m2(b - 1, 0)
+                m2(b - 1, 1)
+                quant("qi", "qc", "qsc", b)
+                if 2 <= b < B - 0:
+                    recip(b - 2)
+                    for mt in range(4):
+                        norm(b - 2, mt, NORM_ENG[mt])
+                if b + 2 < B:
+                    segint(b + 2, SEG_ENG)
+                for j in range(4):
+                    ke(b, j)
+                m2(b - 1, 2)
+                m2(b - 1, 3)
+                for mt in range(4):
+                    xmax(b - 1, mt)
+                    expo(b - 1, mt)
+                if b >= 2:
+                    for c in range(4):
+                        if b == B - 1 and c == 2:
+                            quant("keyi", "keyc", "keys", b)
+                            for mt in range(4):
+                                m2(b, mt)
+                        trans(b - 2, c)
+                        evac(b - 2, c, "s")
+                if b + 2 < B:
+                    widen(b + 2)
+            b = B - 1
+            for mt in range(4):
+                xmax(b, mt)
+                if mt == 0:
+                    recip(b - 1)
+                expo(b, mt)
+            for mt in range(4):
+                norm(b - 1, mt, "gvgv"[mt])
+            recip(b, 0, 2)
+            norm(b, 0, "v")
+            norm(b, 1, "v")
+            for c in range(4):
+                trans(b - 1, c)
+            evac(b - 1, 0, "v")
+            evac(b - 1, 1, "s")
+            recip(b, 2, 4)
+            norm(b, 2, "v")
+            norm(b, 3, "v")
+            evac(b - 1, 2, "v")
+            evac(b - 1, 3, "s")
+            for mt in range(4):
+                tail_store(b, mt, "v,s,v,s".split(",")[mt])

@@ -21,7 +21,7 @@ N = 512
 P = 128
 PACK = 4
 SEGI_BUFS = 3
-SEG_ENG = "gggs"
+SEG_ENG = "gsss"
 NORM_ENG = "gggg"
 FLOPS = 2 * B * C * C * N * 2
 
@@ -91,7 +91,7 @@ def tile_featuremaptransformer_pb_t_w4_kernel(tc, q_bytes, q_scale, seg, w_words
             q1_part(b, 0, N)
 
         def m1(b, j):
-            bank = psum.tile([P, PACK, P], F32, name="bank", tag="bank", bufs=6)
+            bank = psum.tile([P, PACK, P], F32, name="bank", tag="bank", bufs=8)
             T["kb", b, j] = bank
             for t in range(PACK):
                 nc.tensor.matmul_mx(
@@ -145,7 +145,7 @@ def tile_featuremaptransformer_pb_t_w4_kernel(tc, q_bytes, q_scale, seg, w_words
                     nc.gpsimd.tensor_scalar(dst, src, 1.0, 0.0, op0=ALU.mult, op1=ALU.add)
 
         def m2(b, mt):
-            bank = psum.tile([P, N], F32, name="bank", tag="bank", bufs=6)
+            bank = psum.tile([P, N], F32, name="bank", tag="bank", bufs=8)
             T["sb", b, mt] = bank
             nc.tensor.matmul_mx(
                 out=bank[:],
@@ -192,16 +192,13 @@ def tile_featuremaptransformer_pb_t_w4_kernel(tc, q_bytes, q_scale, seg, w_words
                 nc.gpsimd.tensor_scalar(e, e, r, 0.0, op0=ALU.mult, op1=ALU.add)
 
         def trans(b, c):
-            if b == B - 2:
-                bank = psum.tile([P, 4, P], F32, name="bank", tag="bank", bufs=6)
-            else:
-                bank = psum.tile([P, 4, P], F32, name="tbank", tag="tbank", bufs=2)
+            bank = psum.tile([P, 4, P], F32, name="bank", tag="bank", bufs=8)
             T["tb", b, c] = bank
             for mt in range(4):
                 nc.tensor.transpose(bank[:, mt, :], T["e", b][:, mt, P * c : P * (c + 1)], ident[:])
 
         def tail_store(b, mt, eng):
-            bank = psum.tile([P, 4, P], F32, name="bank", tag="bank", bufs=6)
+            bank = psum.tile([P, 4, P], F32, name="bank", tag="bank", bufs=8)
             for c in range(4):
                 nc.tensor.transpose(bank[:, c, :], T["e", b][:, mt, P * c : P * (c + 1)], ident[:])
             o = work.tile([P, 4, P], F32, name="o", tag="o", bufs=8)
@@ -301,15 +298,15 @@ def tile_featuremaptransformer_pb_t_w4_kernel(tc, q_bytes, q_scale, seg, w_words
                     expo(b - 1, mt)
                 if b >= 2:
                     for c in range(4):
-                        if b == B - 1 and c == 2:
-                            quant("keyi", "keyc", "keys", b)
-                            for mt in range(4):
-                                m2(b, mt)
                         trans(b - 2, c)
-                        evac(b - 2, c, "s")
+                        if b < B - 1 or c in (0, 1, 2, 3):
+                            evac(b - 2, c, "s")
                 if b + 2 < B:
                     widen(b + 2)
             b = B - 1
+            quant("keyi", "keyc", "keys", b)
+            for mt in range(4):
+                m2(b, mt)
             for mt in range(4):
                 xmax(b, mt)
                 if mt == 0:
@@ -317,17 +314,20 @@ def tile_featuremaptransformer_pb_t_w4_kernel(tc, q_bytes, q_scale, seg, w_words
                 expo(b, mt)
             for mt in range(4):
                 norm(b - 1, mt, "gvgv"[mt])
-            recip(b, 0, 2)
-            norm(b, 0, "v")
-            norm(b, 1, "v")
+            for c in range(4):
+                if c not in (0, 1, 2, 3):
+                    evac(b - 2, c, "vvvv"[c])
             for c in range(4):
                 trans(b - 1, c)
             evac(b - 1, 0, "v")
-            evac(b - 1, 1, "s")
+            recip(b, 0, 2)
+            norm(b, 0, "v")
+            norm(b, 1, "v")
+            evac(b - 1, 1, "v")
+            evac(b - 1, 2, "s")
             recip(b, 2, 4)
             norm(b, 2, "v")
             norm(b, 3, "v")
-            evac(b - 1, 2, "v")
             evac(b - 1, 3, "s")
             for mt in range(4):
                 tail_store(b, mt, "v,s,v,s".split(",")[mt])

@@ -21,8 +21,8 @@ N = 512
 P = 128
 PACK = 4
 SEGI_BUFS = 3
-SEG_ENG = "gsss"
-NORM_ENG = "gggg"
+ND = 0
+QSB = [128, 192, 0, 0, 0, 0, 0, 0]
 FLOPS = 2 * B * C * C * N * 2
 
 
@@ -72,11 +72,13 @@ def tile_featuremaptransformer_pb_t_w4_kernel(tc, q_bytes, q_scale, seg, w_words
             else:
                 nc.gpsimd.tensor_scalar(dst, src, 1.0, 0.0, op0=ALU.mult, op1=ALU.add)
 
-        def segint(b, eng, parts=4):
+        def segint(b, plan):
             new("segi", b, [P, N, PACK], BF16, bufs=SEGI_BUFS)
-            w = N // parts
-            for k in range(parts):
-                seg_group(b, k * w, (k + 1) * w, eng[k % len(eng)])
+            m = 0
+            for tok in plan.split():
+                w = 64 * int(tok[0])
+                seg_group(b, m, m + w, tok[1])
+                m += w
 
         def q1_part(b, m0, m1):
             nc.vector.quantize_mx(
@@ -122,7 +124,7 @@ def tile_featuremaptransformer_pb_t_w4_kernel(tc, q_bytes, q_scale, seg, w_words
             )
 
         def widen(b):
-            w = new("qw", b, [P, PACK, N], BF16, bufs=3)
+            w = new("qw", b, [P, PACK, N], BF16, bufs=4)
             for t in range(PACK):
                 nc.scalar.activation(
                     out=w[:, t, :],
@@ -130,19 +132,21 @@ def tile_featuremaptransformer_pb_t_w4_kernel(tc, q_bytes, q_scale, seg, w_words
                     func=ACT.Copy,
                     scale=qs[:, t : t + 1],
                 )
+            new("qi", b, [P, N, PACK], BF16, bufs=4)
+            if QSB[b]:
+                qgroup(b, N - QSB[b], N, "s")
+
+        def qgroup(b, m0, m1, eng):
+            dst = T["qi", b][:, m0:m1, :].rearrange("p (c i) t -> p c t i", i=4)
+            src = T["qw", b][:, :, m0:m1].rearrange("p t (c i) -> p c t i", i=4)
+            if eng == "v":
+                nc.vector.tensor_copy(out=dst, in_=src)
+            else:
+                nc.scalar.copy(dst, src)
 
         def qint(b, engs="v"):
-            d = new("qi", b, [P, N, PACK], BF16)
-            w = N // len(engs)
-            for k, e in enumerate(engs):
-                dst = d[:, k * w : (k + 1) * w, :].rearrange("p (c i) t -> p c t i", i=4)
-                src = T["qw", b][:, :, k * w : (k + 1) * w].rearrange("p t (c i) -> p c t i", i=4)
-                if e == "v":
-                    nc.vector.tensor_copy(out=dst, in_=src)
-                elif e == "s":
-                    nc.scalar.copy(dst, src)
-                else:
-                    nc.gpsimd.tensor_scalar(dst, src, 1.0, 0.0, op0=ALU.mult, op1=ALU.add)
+            if QSB[b] < N:
+                qgroup(b, 0, N - QSB[b], "v")
 
         def m2(b, mt):
             bank = psum.tile([P, N], F32, name="bank", tag="bank", bufs=8)
@@ -182,6 +186,9 @@ def tile_featuremaptransformer_pb_t_w4_kernel(tc, q_bytes, q_scale, seg, w_words
             nc.vector.reciprocal(out=T["r", b][:, m0:m1], in_=T["sum", b][:, m0:m1])
 
         def norm(b, mt, eng):
+            if mt < ND and b < B - 1:
+                diag(b, mt)
+                return
             e = T["e", b][:, mt, :]
             r = T["r", b][:, mt : mt + 1]
             if eng == "v":
@@ -191,11 +198,24 @@ def tile_featuremaptransformer_pb_t_w4_kernel(tc, q_bytes, q_scale, seg, w_words
             else:
                 nc.gpsimd.tensor_scalar(e, e, r, 0.0, op0=ALU.mult, op1=ALU.add)
 
+        def diag(b, mt):
+            d = new("diag%d" % mt, b, [P, P], F32)
+            nc.vector.tensor_scalar(d[:], ident[:], T["r", b][:, mt : mt + 1], None, op0=ALU.mult)
+
         def trans(b, c):
             bank = psum.tile([P, 4, P], F32, name="bank", tag="bank", bufs=8)
             T["tb", b, c] = bank
             for mt in range(4):
-                nc.tensor.transpose(bank[:, mt, :], T["e", b][:, mt, P * c : P * (c + 1)], ident[:])
+                if mt < ND:
+                    nc.tensor.matmul(
+                        out=bank[:, mt, :],
+                        lhsT=T["e", b][:, mt, P * c : P * (c + 1)],
+                        rhs=T["diag%d" % mt, b][:],
+                        start=True,
+                        stop=True,
+                    )
+                else:
+                    nc.tensor.transpose(bank[:, mt, :], T["e", b][:, mt, P * c : P * (c + 1)], ident[:])
 
         def tail_store(b, mt, eng):
             bank = psum.tile([P, 4, P], F32, name="bank", tag="bank", bufs=8)
@@ -226,13 +246,16 @@ def tile_featuremaptransformer_pb_t_w4_kernel(tc, q_bytes, q_scale, seg, w_words
             nc.vector.memset(dummy[:], 0.0)
             nc.gpsimd.dma_start(out=qs[:], in_=q_scale.rearrange("o (p t) u -> p (o t u)", t=PACK))
             nc.gpsimd.dma_start(out=bias_b[:], in_=bias.rearrange("(p t) -> p t", t=PACK))
-            load_seg(0, 0, N // 2)
+            if not False:
+                load_seg(0, 0, N // 2)
             nc.sync.dma_start(out=w_raw[:], in_=w_words[0])
             for quad in range(4):
                 nc.sync.dma_start(
                     out=s_raw[32 * quad : 32 * quad + 4, :].bitcast(I32),
                     in_=w_scales[0, 4 * quad : 4 * quad + 4, :].bitcast(I32),
                 )
+            if False:
+                load_seg(0, 0, N // 2)
             load_seg(0, N // 2, N)
             load_q(0)
             for b in range(1, B):
@@ -244,7 +267,10 @@ def tile_featuremaptransformer_pb_t_w4_kernel(tc, q_bytes, q_scale, seg, w_words
             new("segi", 0, [P, N, PACK], BF16, bufs=SEGI_BUFS)
             new("segc", 0, [P, N], U32)
             new("segs", 0, [P, N], U8)
-            seg_group(0, 0, N // 2, "v")
+            hs = "svvs"
+            if not False:
+                seg_group(0, 0, N // 4, hs[0])
+                seg_group(0, N // 4, N // 2, hs[1])
             nc.vector.tensor_copy(
                 out=w_cod[:].rearrange("p (t m e) -> p t m e", t=4, e=2),
                 in_=w_raw[:].rearrange("p (m t e) -> p t m e", t=4, e=2),
@@ -252,8 +278,12 @@ def tile_featuremaptransformer_pb_t_w4_kernel(tc, q_bytes, q_scale, seg, w_words
             nc.vector.tensor_copy(
                 out=w_scl[:].rearrange("p (t m) -> p t m", t=4), in_=s_raw[:].rearrange("p (m t) -> p t m", t=4)
             )
+            if False:
+                seg_group(0, 0, N // 4, hs[0])
+                seg_group(0, N // 4, N // 2, hs[1])
+            seg_group(0, N // 2, 3 * N // 4, hs[2])
+            seg_group(0, 3 * N // 4, N, hs[3])
             q1_part(0, 0, N // 2)
-            seg_group(0, N // 2, N, "v")
             m1(0, 0)
             m1(0, 1)
             q1_part(0, N // 2, N)
@@ -261,62 +291,78 @@ def tile_featuremaptransformer_pb_t_w4_kernel(tc, q_bytes, q_scale, seg, w_words
             m1(0, 3)
             nc.scalar.copy(bias_f[:], bias_b[:])
             widen(0)
-            segint(1, "gggs")
+            segint(1, "4g 4s")
             for j in range(4):
                 ke(0, j)
-            qint(0, "v")
+            qint(0)
             widen(1)
-            segint(2, SEG_ENG)
+            segint(2, "4s 4v")
             widen(2)
-            quant("qi", "qc", "qsc", 0)
+            if True:
+                quant("keyi", "keyc", "keys", 0)
+                quant("qi", "qc", "qsc", 0)
+                for mt in range(4):
+                    m2(0, mt)
+            else:
+                quant("qi", "qc", "qsc", 0)
 
             for b in range(1, B):
                 q1(b)
                 for j in range(4):
                     m1(b, j)
-                qint(b, "v")
-                if b >= B - 0:
+                if b == 1 and True:
+                    for mt in range(4):
+                        xmax(0, mt)
+                        expo(0, mt)
+                qint(b)
+                if b > 1 or not True:
+                    quant("keyi", "keyc", "keys", b - 1)
+                    for mt in range(4):
+                        m2(b - 1, mt)
+                if b >= B - 1:
                     recip(b - 2)
                     for mt in range(4):
-                        norm(b - 2, mt, "ssss"[mt])
-                quant("keyi", "keyc", "keys", b - 1)
-                m2(b - 1, 0)
-                m2(b - 1, 1)
+                        norm(b - 2, mt, "sgsg"[mt])
                 quant("qi", "qc", "qsc", b)
-                if 2 <= b < B - 0:
+                if b >= 2 and b < B - 1:
                     recip(b - 2)
-                    for mt in range(4):
-                        norm(b - 2, mt, NORM_ENG[mt])
-                if b + 2 < B:
-                    segint(b + 2, SEG_ENG)
+                if b >= 2 or b + 2 < B:
+                    k = 0
+                    for g in ["snnnn", "snnnn", "snnnn", "snnnn", "snnnn", "nnnn", "nnnn"][b - 1]:
+                        if g == "n":
+                            if b >= 2 and b < B - 1:
+                                norm(b - 2, k, ["gggg", "gggg", "gggg", "gggg", "gggg", "gggg"][b - 2][k])
+                            k += 1
+                        elif b + 2 < B:
+                            segint(b + 2, ["2g 5s 1v", "2g 5s 1v", "2g 5s 1v", "2g 5s 1v", "2g 5s 1v"][b - 1])
                 for j in range(4):
                     ke(b, j)
-                m2(b - 1, 2)
-                m2(b - 1, 3)
-                for mt in range(4):
-                    xmax(b - 1, mt)
-                    expo(b - 1, mt)
+                if b > 1 or not True:
+                    for mt in range(4):
+                        xmax(b - 1, mt)
+                        expo(b - 1, mt)
+                if b == B - 1 and False:
+                    quant("keyi", "keyc", "keys", b)
+                    for mt in range(4):
+                        m2(b, mt)
                 if b >= 2:
                     for c in range(4):
                         trans(b - 2, c)
-                        if b < B - 1 or c in (0, 1, 2, 3):
-                            evac(b - 2, c, "s")
+                        evac(b - 2, c, "s")
                 if b + 2 < B:
                     widen(b + 2)
             b = B - 1
-            quant("keyi", "keyc", "keys", b)
-            for mt in range(4):
-                m2(b, mt)
+            if not False:
+                quant("keyi", "keyc", "keys", b)
+                for mt in range(4):
+                    m2(b, mt)
             for mt in range(4):
                 xmax(b, mt)
                 if mt == 0:
                     recip(b - 1)
                 expo(b, mt)
             for mt in range(4):
-                norm(b - 1, mt, "gvgv"[mt])
-            for c in range(4):
-                if c not in (0, 1, 2, 3):
-                    evac(b - 2, c, "vvvv"[c])
+                norm(b - 1, mt, "ggvv"[mt])
             for c in range(4):
                 trans(b - 1, c)
             evac(b - 1, 0, "v")
@@ -330,4 +376,4 @@ def tile_featuremaptransformer_pb_t_w4_kernel(tc, q_bytes, q_scale, seg, w_words
             norm(b, 3, "v")
             evac(b - 1, 3, "s")
             for mt in range(4):
-                tail_store(b, mt, "v,s,v,s".split(",")[mt])
+                tail_store(b, mt, "s,v,s,v".split(",")[mt])

@@ -20,9 +20,8 @@ C = 512
 N = 512
 P = 128
 PACK = 4
-SEGI_BUFS = 3
-ND = 0
-QSB = [128, 192, 0, 0, 0, 0, 0, 0]
+SEGI_BUFS = 4
+QSB = [256, 256, 160, 160, 160, 160, 160, 160]
 FLOPS = 2 * B * C * C * N * 2
 
 
@@ -186,8 +185,9 @@ def tile_featuremaptransformer_pb_t_w4_kernel(tc, q_bytes, q_scale, seg, w_words
             nc.vector.reciprocal(out=T["r", b][:, m0:m1], in_=T["sum", b][:, m0:m1])
 
         def norm(b, mt, eng):
-            if mt < ND and b < B - 1:
+            if eng == "d":
                 diag(b, mt)
+                T["isd", b, mt] = 1
                 return
             e = T["e", b][:, mt, :]
             r = T["r", b][:, mt : mt + 1]
@@ -202,11 +202,14 @@ def tile_featuremaptransformer_pb_t_w4_kernel(tc, q_bytes, q_scale, seg, w_words
             d = new("diag%d" % mt, b, [P, P], F32)
             nc.vector.tensor_scalar(d[:], ident[:], T["r", b][:, mt : mt + 1], None, op0=ALU.mult)
 
-        def trans(b, c):
-            bank = psum.tile([P, 4, P], F32, name="bank", tag="bank", bufs=8)
-            T["tb", b, c] = bank
+        def trans_part(b, c, kind):
+            if ("tb", b, c) not in T:
+                T["tb", b, c] = None
+                bank = psum.tile([P, 4, P], F32, name="bank", tag="bank", bufs=8)
+                T["tb", b, c] = bank
+            bank = T["tb", b, c]
             for mt in range(4):
-                if mt < ND:
+                if kind == "d" and ("isd", b, mt) in T:
                     nc.tensor.matmul(
                         out=bank[:, mt, :],
                         lhsT=T["e", b][:, mt, P * c : P * (c + 1)],
@@ -214,8 +217,13 @@ def tile_featuremaptransformer_pb_t_w4_kernel(tc, q_bytes, q_scale, seg, w_words
                         start=True,
                         stop=True,
                     )
-                else:
+                if kind == "t" and ("isd", b, mt) not in T:
                     nc.tensor.transpose(bank[:, mt, :], T["e", b][:, mt, P * c : P * (c + 1)], ident[:])
+
+        def trans(b):
+            for kind in "dt":
+                for c in range(4):
+                    trans_part(b, c, kind)
 
         def tail_store(b, mt, eng):
             bank = psum.tile([P, 4, P], F32, name="bank", tag="bank", bufs=8)
@@ -246,7 +254,7 @@ def tile_featuremaptransformer_pb_t_w4_kernel(tc, q_bytes, q_scale, seg, w_words
             nc.vector.memset(dummy[:], 0.0)
             nc.gpsimd.dma_start(out=qs[:], in_=q_scale.rearrange("o (p t) u -> p (o t u)", t=PACK))
             nc.gpsimd.dma_start(out=bias_b[:], in_=bias.rearrange("(p t) -> p t", t=PACK))
-            if not False:
+            if not True:
                 load_seg(0, 0, N // 2)
             nc.sync.dma_start(out=w_raw[:], in_=w_words[0])
             for quad in range(4):
@@ -254,7 +262,7 @@ def tile_featuremaptransformer_pb_t_w4_kernel(tc, q_bytes, q_scale, seg, w_words
                     out=s_raw[32 * quad : 32 * quad + 4, :].bitcast(I32),
                     in_=w_scales[0, 4 * quad : 4 * quad + 4, :].bitcast(I32),
                 )
-            if False:
+            if True:
                 load_seg(0, 0, N // 2)
             load_seg(0, N // 2, N)
             load_q(0)
@@ -267,8 +275,8 @@ def tile_featuremaptransformer_pb_t_w4_kernel(tc, q_bytes, q_scale, seg, w_words
             new("segi", 0, [P, N, PACK], BF16, bufs=SEGI_BUFS)
             new("segc", 0, [P, N], U32)
             new("segs", 0, [P, N], U8)
-            hs = "svvs"
-            if not False:
+            hs = "vsvs"
+            if not True:
                 seg_group(0, 0, N // 4, hs[0])
                 seg_group(0, N // 4, N // 2, hs[1])
             nc.vector.tensor_copy(
@@ -278,7 +286,7 @@ def tile_featuremaptransformer_pb_t_w4_kernel(tc, q_bytes, q_scale, seg, w_words
             nc.vector.tensor_copy(
                 out=w_scl[:].rearrange("p (t m) -> p t m", t=4), in_=s_raw[:].rearrange("p (m t) -> p t m", t=4)
             )
-            if False:
+            if True:
                 seg_group(0, 0, N // 4, hs[0])
                 seg_group(0, N // 4, N // 2, hs[1])
             seg_group(0, N // 2, 3 * N // 4, hs[2])
@@ -319,22 +327,27 @@ def tile_featuremaptransformer_pb_t_w4_kernel(tc, q_bytes, q_scale, seg, w_words
                     quant("keyi", "keyc", "keys", b - 1)
                     for mt in range(4):
                         m2(b - 1, mt)
-                if b >= B - 1:
+                if b >= B - 2:
                     recip(b - 2)
                     for mt in range(4):
-                        norm(b - 2, mt, "sgsg"[mt])
+                        norm(b - 2, mt, "gggg"[mt])
+                nd = "ddgg".count("d") if 2 <= b < B - 2 else 0
+                if nd:
+                    recip(b - 2, 0, nd)
                 quant("qi", "qc", "qsc", b)
-                if b >= 2 and b < B - 1:
-                    recip(b - 2)
+                if 2 <= b < B - 2:
+                    for k in range(nd):
+                        norm(b - 2, k, "d")
+                    recip(b - 2, nd, 4)
                 if b >= 2 or b + 2 < B:
                     k = 0
-                    for g in ["snnnn", "snnnn", "snnnn", "snnnn", "snnnn", "nnnn", "nnnn"][b - 1]:
+                    for g in ["nnnsn", "nnnsn", "nnnsn", "nnnsn", "nnnsn", "nnnn", "nnnn"][b - 1]:
                         if g == "n":
-                            if b >= 2 and b < B - 1:
-                                norm(b - 2, k, ["gggg", "gggg", "gggg", "gggg", "gggg", "gggg"][b - 2][k])
+                            if b >= 2 and b < B - 2 and k >= nd:
+                                norm(b - 2, k, ["ddgg", "ddgg", "ddgg", "ddgg", "ddgg", "ddgg"][b - 2][k])
                             k += 1
                         elif b + 2 < B:
-                            segint(b + 2, ["2g 5s 1v", "2g 5s 1v", "2g 5s 1v", "2g 5s 1v", "2g 5s 1v"][b - 1])
+                            segint(b + 2, ["8g", "8g", "8g", "8g", "8g"][b - 1])
                 for j in range(4):
                     ke(b, j)
                 if b > 1 or not True:
@@ -346,8 +359,8 @@ def tile_featuremaptransformer_pb_t_w4_kernel(tc, q_bytes, q_scale, seg, w_words
                     for mt in range(4):
                         m2(b, mt)
                 if b >= 2:
+                    trans(b - 2)
                     for c in range(4):
-                        trans(b - 2, c)
                         evac(b - 2, c, "s")
                 if b + 2 < B:
                     widen(b + 2)
@@ -363,8 +376,7 @@ def tile_featuremaptransformer_pb_t_w4_kernel(tc, q_bytes, q_scale, seg, w_words
                 expo(b, mt)
             for mt in range(4):
                 norm(b - 1, mt, "ggvv"[mt])
-            for c in range(4):
-                trans(b - 1, c)
+            trans(b - 1)
             evac(b - 1, 0, "v")
             recip(b, 0, 2)
             norm(b, 0, "v")
@@ -376,4 +388,4 @@ def tile_featuremaptransformer_pb_t_w4_kernel(tc, q_bytes, q_scale, seg, w_words
             norm(b, 3, "v")
             evac(b - 1, 3, "s")
             for mt in range(4):
-                tail_store(b, mt, "s,v,s,v".split(",")[mt])
+                tail_store(b, mt, "v,s,v,vs".split(",")[mt])

@@ -21,7 +21,7 @@ N = 512
 P = 128
 PACK = 4
 SEGI_BUFS = 4
-QSB = [256, 256, 160, 160, 160, 160, 160, 160]
+QSB = [192, 256, 0, 0, 0, 0, 0, 0]
 FLOPS = 2 * B * C * C * N * 2
 
 
@@ -225,6 +225,28 @@ def tile_featuremaptransformer_pb_t_w4_kernel(tc, q_bytes, q_scale, seg, w_words
                 for c in range(4):
                     trans_part(b, c, kind)
 
+        def tail_store2(b, pair, half, eng):
+            bank = psum.tile([P, 2, 2 * P], F32, name="bank", tag="bank", bufs=8)
+            for k in range(2):
+                c = 2 * half + k
+                for u in range(2):
+                    mt = 2 * pair + u
+                    nc.tensor.transpose(
+                        bank[:, k, P * u : P * (u + 1)], T["e", b][:, mt, P * c : P * (c + 1)], ident[:]
+                    )
+            o = work.tile([P, 2, 2 * P], F32, name="o", tag="o", bufs=8)
+            dst = out[b].rearrange("(c p) m -> p c m", p=P)
+            for k, e in enumerate(eng):
+                w = 2 // len(eng)
+                ks = slice(k * w, (k + 1) * w)
+                if e == "s":
+                    nc.scalar.copy(o[:, ks, :], bank[:, ks, :])
+                else:
+                    nc.vector.tensor_copy(out=o[:, ks, :], in_=bank[:, ks, :])
+                nc.sync.dma_start(
+                    out=dst[:, 2 * half + k * w : 2 * half + (k + 1) * w, 2 * P * pair : 2 * P * (pair + 1)], in_=o[:, ks, :]
+                )
+
         def tail_store(b, mt, eng):
             bank = psum.tile([P, 4, P], F32, name="bank", tag="bank", bufs=8)
             for c in range(4):
@@ -254,18 +276,29 @@ def tile_featuremaptransformer_pb_t_w4_kernel(tc, q_bytes, q_scale, seg, w_words
             nc.vector.memset(dummy[:], 0.0)
             nc.gpsimd.dma_start(out=qs[:], in_=q_scale.rearrange("o (p t) u -> p (o t u)", t=PACK))
             nc.gpsimd.dma_start(out=bias_b[:], in_=bias.rearrange("(p t) -> p t", t=PACK))
-            if not True:
-                load_seg(0, 0, N // 2)
-            nc.sync.dma_start(out=w_raw[:], in_=w_words[0])
-            for quad in range(4):
-                nc.sync.dma_start(
-                    out=s_raw[32 * quad : 32 * quad + 4, :].bitcast(I32),
-                    in_=w_scales[0, 4 * quad : 4 * quad + 4, :].bitcast(I32),
-                )
-            if True:
-                load_seg(0, 0, N // 2)
-            load_seg(0, N // 2, N)
-            load_q(0)
+            def load_w():
+                nc.sync.dma_start(out=w_raw[:], in_=w_words[0])
+
+            def load_s():
+                for quad in range(4):
+                    nc.sync.dma_start(
+                        out=s_raw[32 * quad : 32 * quad + 4, :].bitcast(I32),
+                        in_=w_scales[0, 4 * quad : 4 * quad + 4, :].bitcast(I32),
+                    )
+
+            for tok in "S W f q".split():
+                if tok == "W":
+                    load_w()
+                elif tok == "S":
+                    load_s()
+                elif tok == "a":
+                    load_seg(0, 0, N // 2)
+                elif tok == "b":
+                    load_seg(0, N // 2, N)
+                elif tok == "f":
+                    load_seg(0, 0, N)
+                elif tok == "q":
+                    load_q(0)
             for b in range(1, B):
                 load_seg(b, 0, N)
                 load_q(b)
@@ -299,7 +332,7 @@ def tile_featuremaptransformer_pb_t_w4_kernel(tc, q_bytes, q_scale, seg, w_words
             m1(0, 3)
             nc.scalar.copy(bias_f[:], bias_b[:])
             widen(0)
-            segint(1, "4g 4s")
+            segint(1, "4g 2g 2s")
             for j in range(4):
                 ke(0, j)
             qint(0)
@@ -327,27 +360,27 @@ def tile_featuremaptransformer_pb_t_w4_kernel(tc, q_bytes, q_scale, seg, w_words
                     quant("keyi", "keyc", "keys", b - 1)
                     for mt in range(4):
                         m2(b - 1, mt)
-                if b >= B - 2:
+                if b >= B - 1:
                     recip(b - 2)
                     for mt in range(4):
-                        norm(b - 2, mt, "gggg"[mt])
-                nd = "ddgg".count("d") if 2 <= b < B - 2 else 0
+                        norm(b - 2, mt, "ggss"[mt])
+                nd = "gggg".count("d") if 2 <= b < B - 1 else 0
                 if nd:
                     recip(b - 2, 0, nd)
                 quant("qi", "qc", "qsc", b)
-                if 2 <= b < B - 2:
+                if 2 <= b < B - 1:
                     for k in range(nd):
                         norm(b - 2, k, "d")
                     recip(b - 2, nd, 4)
                 if b >= 2 or b + 2 < B:
                     k = 0
-                    for g in ["nnnsn", "nnnsn", "nnnsn", "nnnsn", "nnnsn", "nnnn", "nnnn"][b - 1]:
+                    for g in ["snnnn", "snnnn", "snnnn", "snnnn", "snnnn", "nnnn", "nnnn"][b - 1]:
                         if g == "n":
-                            if b >= 2 and b < B - 2 and k >= nd:
-                                norm(b - 2, k, ["ddgg", "ddgg", "ddgg", "ddgg", "ddgg", "ddgg"][b - 2][k])
+                            if b >= 2 and b < B - 1 and k >= nd:
+                                norm(b - 2, k, ["gggg", "gggg", "gggg", "gggg", "gggg", "gggg"][b - 2][k])
                             k += 1
                         elif b + 2 < B:
-                            segint(b + 2, ["8g", "8g", "8g", "8g", "8g"][b - 1])
+                            segint(b + 2, ["2g 5s 1v", "2g 5s 1v", "2g 5s 1v", "2g 5s 1v", "2g 5s 1v"][b - 1])
                 for j in range(4):
                     ke(b, j)
                 if b > 1 or not True:
@@ -375,17 +408,21 @@ def tile_featuremaptransformer_pb_t_w4_kernel(tc, q_bytes, q_scale, seg, w_words
                     recip(b - 1)
                 expo(b, mt)
             for mt in range(4):
-                norm(b - 1, mt, "ggvv"[mt])
+                norm(b - 1, mt, "vgvg"[mt])
             trans(b - 1)
-            evac(b - 1, 0, "v")
             recip(b, 0, 2)
             norm(b, 0, "v")
             norm(b, 1, "v")
-            evac(b - 1, 1, "v")
-            evac(b - 1, 2, "s")
+            evac(b - 1, 0, "v")
+            evac(b - 1, 1, "s")
+            evac(b - 1, 2, "v")
             recip(b, 2, 4)
             norm(b, 2, "v")
             norm(b, 3, "v")
             evac(b - 1, 3, "s")
-            for mt in range(4):
-                tail_store(b, mt, "v,s,v,vs".split(",")[mt])
+            if 2 == 1:
+                for mt in range(4):
+                    tail_store(b, mt, "s,v,v,s".split(",")[mt])
+            else:
+                for k in range(4):
+                    tail_store2(b, k // 2, k % 2, "s,v,v,s".split(",")[k])

from contextlib import ExitStack

import concourse.mybir as mybir
from concourse.masks import make_identity

F32 = mybir.dt.float32
BF16 = mybir.dt.bfloat16
I32 = mybir.dt.int32
U32 = mybir.dt.uint32
U8 = mybir.dt.uint8
FP8 = mybir.dt.float8_e4m3fn
FP8X4 = mybir.dt.float8_e4m3fn_x4
FP4X4 = mybir.dt.float4_e2m1fn_x4
ACT = mybir.ActivationFunctionType
ALU = mybir.AluOpType
AX = mybir.AxisListType

B = 8
C = 512
N = 512
P = 128
PACK = 4
SEGI_BUFS = 4
QSB = [192, 256, 0, 0, 0, 0, 0, 0]
FLOPS = 2 * B * C * C * N * 2


def tile_featuremaptransformer_pb_t_w4_kernel(tc, q_bytes, q_scale, seg, w_words, w_scales, bias, out):
    nc = tc.nc
    seg_v = seg.rearrange("b (p t) h w -> b p t (h w)", t=PACK)
    q_v = q_bytes.rearrange("b (p t) n -> b p (t n)", t=PACK)

    with ExitStack() as ctx:
        keep = ctx.enter_context(tc.tile_pool(name="keep", bufs=1))
        work = ctx.enter_context(tc.tile_pool(name="work", bufs=2))
        psum = ctx.enter_context(tc.psum_pool(name="psum", bufs=1))

        w_raw = keep.tile([P, 2 * C], U8, name="w_raw", align_bytes=64)
        w_cod = keep.tile([P, 2 * C], U8, name="w_cod", align_bytes=64)
        s_raw = keep.tile([P, C], U8, name="s_raw", align_bytes=64)
        w_scl = keep.tile([P, C], U8, name="w_scl", align_bytes=64)
        bias_b = keep.tile([P, PACK], BF16, name="bias_b")
        bias_f = keep.tile([P, PACK], F32, name="bias_f")
        qs = keep.tile([P, PACK], F32, name="qs")
        ident = keep.tile([P, P], F32, name="ident")
        dummy = keep.tile([P, 1], F32, name="dummy")
        seg_raw = [keep.tile([P, PACK, N], BF16, name="seg_raw%d" % b, align_bytes=64) for b in range(B)]
        q_raw = [keep.tile([P, PACK * N], U8, name="q_raw%d" % b, align_bytes=64) for b in range(B)]

        T = {}

        def load_seg(b, m0, m1):
            nc.sync.dma_start(out=seg_raw[b][:, :, m0:m1], in_=seg_v[b][:, :, m0:m1])

        def load_q(b):
            nc.sync.dma_start(out=q_raw[b][:], in_=q_v[b])

        def new(key, b, shape, dt, bufs=2):
            t = work.tile(shape, dt, name=key, tag=key, bufs=bufs, align_bytes=64)
            T[key, b] = t
            return t

        def seg_group(b, m0, m1, eng):
            t = T["segi", b]
            dst = t[:, m0:m1, :].rearrange("p (c i) t -> p c t i", i=4)
            src = seg_raw[b][:, :, m0:m1].rearrange("p t (c i) -> p c t i", i=4)
            if eng == "v":
                nc.vector.tensor_copy(out=dst, in_=src)
            elif eng == "s":
                nc.scalar.copy(dst, src)
            else:
                nc.gpsimd.tensor_scalar(dst, src, 1.0, 0.0, op0=ALU.mult, op1=ALU.add)

        def segint(b, plan):
            new("segi", b, [P, N, PACK], BF16, bufs=SEGI_BUFS)
            m = 0
            for tok in plan.split():
                w = 64 * int(tok[0])
                seg_group(b, m, m + w, tok[1])
                m += w

        def q1_part(b, m0, m1):
            nc.vector.quantize_mx(
                out=T["segc", b][:, m0:m1].bitcast(FP8X4),
                scales=T["segs", b][:, m0:m1],
                in_=T["segi", b][:, m0:m1, :].rearrange("p n t -> p (n t)"),
            )

        def q1(b):
            new("segc", b, [P, N], U32)
            new("segs", b, [P, N], U8)
            q1_part(b, 0, N)

        def m1(b, j):
            bank = psum.tile([P, PACK, P], F32, name="bank", tag="bank", bufs=8)
            T["kb", b, j] = bank
            for t in range(PACK):
                nc.tensor.matmul_mx(
                    out=bank[:, t, :],
                    lhsT=w_cod[:, 2 * P * t : 2 * P * (t + 1)].bitcast(FP4X4),
                    lhsT_scale=w_scl[:, P * t : P * (t + 1)],
                    rhs=T["segc", b][:, P * j : P * (j + 1)].bitcast(FP8X4),
                    rhs_scale=T["segs", b][:, P * j : P * (j + 1)],
                    start=True,
                    stop=True,
                )

        def ke(b, j):
            if j == 0:
                new("keyi", b, [P, N, PACK], BF16)
            nc.vector.tensor_tensor(
                out=T["keyi", b][:, P * j : P * (j + 1), :],
                in0=T["kb", b, j][:].rearrange("p t n -> p n t"),
                in1=bias_f[:].unsqueeze(1).to_broadcast([P, P, PACK]),
                op=ALU.add,
            )

        def quant(src, cod, scl, b):
            c = new(cod, b, [P, N], U32)
            s = new(scl, b, [P, N], U8)
            nc.vector.quantize_mx(
                out=c[:].bitcast(FP8X4), scales=s[:], in_=T[src, b][:].rearrange("p n t -> p (n t)")
            )

        def widen(b):
            w = new("qw", b, [P, PACK, N], BF16, bufs=4)
            for t in range(PACK):
                nc.scalar.activation(
                    out=w[:, t, :],
                    in_=q_raw[b][:, N * t : N * (t + 1)].bitcast(FP8),
                    func=ACT.Copy,
                    scale=qs[:, t : t + 1],
                )
            new("qi", b, [P, N, PACK], BF16, bufs=4)
            if QSB[b]:
                qgroup(b, N - QSB[b], N, "s")

        def qgroup(b, m0, m1, eng):
            dst = T["qi", b][:, m0:m1, :].rearrange("p (c i) t -> p c t i", i=4)
            src = T["qw", b][:, :, m0:m1].rearrange("p t (c i) -> p c t i", i=4)
            if eng == "v":
                nc.vector.tensor_copy(out=dst, in_=src)
            else:
                nc.scalar.copy(dst, src)

        def qint(b, engs="v"):
            if QSB[b] < N:
                qgroup(b, 0, N - QSB[b], "v")

        def m2(b, mt):
            bank = psum.tile([P, N], F32, name="bank", tag="bank", bufs=8)
            T["sb", b, mt] = bank
            nc.tensor.matmul_mx(
                out=bank[:],
                lhsT=T["keyc", b][:, P * mt : P * (mt + 1)].bitcast(FP8X4),
                lhsT_scale=T["keys", b][:, P * mt : P * (mt + 1)],
                rhs=T["qc", b][:].bitcast(FP8X4),
                rhs_scale=T["qsc", b][:],
                start=True,
                stop=True,
            )

        def xmax(b, mt):
            if mt == 0:
                new("nmax", b, [P, 4], F32, bufs=3)
            nc.vector.tensor_reduce(
                out=T["nmax", b][:, mt : mt + 1], in_=T["sb", b, mt][:], axis=AX.X, op=ALU.max, negate=True
            )

        def expo(b, mt):
            if mt == 0:
                new("sum", b, [P, 4], F32, bufs=3)
                new("e", b, [P, 4, N], F32, bufs=3)
            nc.scalar.activation(
                out=T["e", b][:, mt, :],
                in_=T["sb", b, mt][:],
                func=ACT.Exp,
                bias=T["nmax", b][:, mt : mt + 1],
                accum_out=T["sum", b][:, mt : mt + 1],
            )

        def recip(b, m0=0, m1=4):
            if m0 == 0:
                new("r", b, [P, 4], F32, bufs=3)
            nc.vector.reciprocal(out=T["r", b][:, m0:m1], in_=T["sum", b][:, m0:m1])

        def norm(b, mt, eng):
            if eng == "d":
                diag(b, mt)
                T["isd", b, mt] = 1
                return
            e = T["e", b][:, mt, :]
            r = T["r", b][:, mt : mt + 1]
            if eng == "v":
                nc.vector.tensor_scalar(e, e, r, None, op0=ALU.mult)
            elif eng == "s":
                nc.scalar.activation(out=e, in_=e, func=ACT.Copy, scale=r)
            else:
                nc.gpsimd.tensor_scalar(e, e, r, 0.0, op0=ALU.mult, op1=ALU.add)

        def diag(b, mt):
            d = new("diag%d" % mt, b, [P, P], F32)
            nc.vector.tensor_scalar(d[:], ident[:], T["r", b][:, mt : mt + 1], None, op0=ALU.mult)

        def trans_part(b, c, kind):
            if ("tb", b, c) not in T:
                T["tb", b, c] = None
                bank = psum.tile([P, 4, P], F32, name="bank", tag="bank", bufs=8)
                T["tb", b, c] = bank
            bank = T["tb", b, c]
            for mt in range(4):
                if kind == "d" and ("isd", b, mt) in T:
                    nc.tensor.matmul(
                        out=bank[:, mt, :],
                        lhsT=T["e", b][:, mt, P * c : P * (c + 1)],
                        rhs=T["diag%d" % mt, b][:],
                        start=True,
                        stop=True,
                    )
                if kind == "t" and ("isd", b, mt) not in T:
                    nc.tensor.transpose(bank[:, mt, :], T["e", b][:, mt, P * c : P * (c + 1)], ident[:])

        def trans(b):
            for kind in "dt":
                for c in range(4):
                    trans_part(b, c, kind)

        def tail_store2(b, pair, half, eng):
            bank = psum.tile([P, 2, 2 * P], F32, name="bank", tag="bank", bufs=8)
            for k in range(2):
                c = 2 * half + k
                for u in range(2):
                    mt = 2 * pair + u
                    nc.tensor.transpose(
                        bank[:, k, P * u : P * (u + 1)], T["e", b][:, mt, P * c : P * (c + 1)], ident[:]
                    )
            o = work.tile([P, 2, 2 * P], F32, name="o", tag="o", bufs=8)
            dst = out[b].rearrange("(c p) m -> p c m", p=P)
            for k, e in enumerate(eng):
                w = 2 // len(eng)
                ks = slice(k * w, (k + 1) * w)
                if e == "s":
                    nc.scalar.copy(o[:, ks, :], bank[:, ks, :])
                else:
                    nc.vector.tensor_copy(out=o[:, ks, :], in_=bank[:, ks, :])
                nc.sync.dma_start(
                    out=dst[:, 2 * half + k * w : 2 * half + (k + 1) * w, 2 * P * pair : 2 * P * (pair + 1)], in_=o[:, ks, :]
                )

        def tail_store(b, mt, eng):
            bank = psum.tile([P, 4, P], F32, name="bank", tag="bank", bufs=8)
            for c in range(4):
                nc.tensor.transpose(bank[:, c, :], T["e", b][:, mt, P * c : P * (c + 1)], ident[:])
            o = work.tile([P, 4, P], F32, name="o", tag="o", bufs=8)
            dst = out[b].rearrange("(c p) m -> p c m", p=P)
            for k, e in enumerate(eng):
                w = 4 // len(eng)
                cs = slice(k * w, (k + 1) * w)
                if e == "s":
                    nc.scalar.copy(o[:, cs, :], bank[:, cs, :])
                else:
                    nc.vector.tensor_copy(out=o[:, cs, :], in_=bank[:, cs, :])
                nc.sync.dma_start(out=dst[:, cs, P * mt : P * (mt + 1)], in_=o[:, cs, :])

        def evac(b, c, eng):
            o = work.tile([P, N], F32, name="o", tag="o", bufs=8)
            src = T["tb", b, c][:].rearrange("p t m -> p (t m)")
            if eng == "s":
                nc.scalar.copy(o[:], src)
            else:
                nc.vector.tensor_copy(out=o[:], in_=src)
            nc.sync.dma_start(out=out[b, P * c : P * (c + 1), :], in_=o[:])

        with tc.manual_schedule():
            nc.vector.memset(s_raw[:].bitcast(I32), 0)
            nc.vector.memset(dummy[:], 0.0)
            nc.gpsimd.dma_start(out=qs[:], in_=q_scale.rearrange("o (p t) u -> p (o t u)", t=PACK))
            nc.gpsimd.dma_start(out=bias_b[:], in_=bias.rearrange("(p t) -> p t", t=PACK))
            def load_w():
                nc.sync.dma_start(out=w_raw[:], in_=w_words[0])

            def load_s():
                for quad in range(4):
                    nc.sync.dma_start(
                        out=s_raw[32 * quad : 32 * quad + 4, :].bitcast(I32),
                        in_=w_scales[0, 4 * quad : 4 * quad + 4, :].bitcast(I32),
                    )

            for tok in "S W f q".split():
                if tok == "W":
                    load_w()
                elif tok == "S":
                    load_s()
                elif tok == "a":
                    load_seg(0, 0, N // 2)
                elif tok == "b":
                    load_seg(0, N // 2, N)
                elif tok == "f":
                    load_seg(0, 0, N)
                elif tok == "q":
                    load_q(0)
            for b in range(1, B):
                load_seg(b, 0, N)
                load_q(b)
            nc.scalar.activation(out=dummy[:], in_=dummy[:], func=ACT.Exp)
            make_identity(nc, ident[:])

            new("segi", 0, [P, N, PACK], BF16, bufs=SEGI_BUFS)
            new("segc", 0, [P, N], U32)
            new("segs", 0, [P, N], U8)
            hs = "vsvs"
            if not True:
                seg_group(0, 0, N // 4, hs[0])
                seg_group(0, N // 4, N // 2, hs[1])
            nc.vector.tensor_copy(
                out=w_cod[:].rearrange("p (t m e) -> p t m e", t=4, e=2),
                in_=w_raw[:].rearrange("p (m t e) -> p t m e", t=4, e=2),
            )
            nc.vector.tensor_copy(
                out=w_scl[:].rearrange("p (t m) -> p t m", t=4), in_=s_raw[:].rearrange("p (m t) -> p t m", t=4)
            )
            if True:
                seg_group(0, 0, N // 4, hs[0])
                seg_group(0, N // 4, N // 2, hs[1])
            seg_group(0, N // 2, 3 * N // 4, hs[2])
            seg_group(0, 3 * N // 4, N, hs[3])
            q1_part(0, 0, N // 2)
            m1(0, 0)
            m1(0, 1)
            q1_part(0, N // 2, N)
            m1(0, 2)
            m1(0, 3)
            nc.scalar.copy(bias_f[:], bias_b[:])
            widen(0)
            segint(1, "4g 2g 2s")
            for j in range(4):
                ke(0, j)
            qint(0)
            widen(1)
            segint(2, "4s 4v")
            widen(2)
            if True:
                quant("keyi", "keyc", "keys", 0)
                quant("qi", "qc", "qsc", 0)
                for mt in range(4):
                    m2(0, mt)
            else:
                quant("qi", "qc", "qsc", 0)

            for b in range(1, B):
                q1(b)
                for j in range(4):
                    m1(b, j)
                if b == 1 and True:
                    for mt in range(4):
                        xmax(0, mt)
                        expo(0, mt)
                qint(b)
                if b > 1 or not True:
                    quant("keyi", "keyc", "keys", b - 1)
                    for mt in range(4):
                        m2(b - 1, mt)
                if b >= B - 1:
                    recip(b - 2)
                    for mt in range(4):
                        norm(b - 2, mt, "ggss"[mt])
                nd = "gggg".count("d") if 2 <= b < B - 1 else 0
                if nd:
                    recip(b - 2, 0, nd)
                quant("qi", "qc", "qsc", b)
                if 2 <= b < B - 1:
                    for k in range(nd):
                        norm(b - 2, k, "d")
                    recip(b - 2, nd, 4)
                if b >= 2 or b + 2 < B:
                    k = 0
                    for g in ["snnnn", "snnnn", "snnnn", "snnnn", "snnnn", "nnnn", "nnnn"][b - 1]:
                        if g == "n":
                            if b >= 2 and b < B - 1 and k >= nd:
                                norm(b - 2, k, ["gggg", "gggg", "gggg", "gggg", "gggg", "gggg"][b - 2][k])
                            k += 1
                        elif b + 2 < B:
                            segint(b + 2, ["2g 5s 1v", "2g 5s 1v", "2g 5s 1v", "2g 5s 1v", "2g 5s 1v"][b - 1])
                for j in range(4):
                    ke(b, j)
                if b > 1 or not True:
                    for mt in range(4):
                        xmax(b - 1, mt)
                        expo(b - 1, mt)
                if b == B - 1 and False:
                    quant("keyi", "keyc", "keys", b)
                    for mt in range(4):
                        m2(b, mt)
                if b >= 2:
                    trans(b - 2)
                    for c in range(4):
                        evac(b - 2, c, "s")
                if b + 2 < B:
                    widen(b + 2)
            b = B - 1
            if not False:
                quant("keyi", "keyc", "keys", b)
                for mt in range(4):
                    m2(b, mt)
            for mt in range(4):
                xmax(b, mt)
                if mt == 0:
                    recip(b - 1)
                expo(b, mt)
            for mt in range(4):
                norm(b - 1, mt, "vgvg"[mt])
            trans(b - 1)
            recip(b, 0, 2)
            norm(b, 0, "v")
            norm(b, 1, "v")
            evac(b - 1, 0, "v")
            evac(b - 1, 1, "s")
            evac(b - 1, 2, "v")
            recip(b, 2, 4)
            norm(b, 2, "v")
            norm(b, 3, "v")
            evac(b - 1, 3, "s")
            if 2 == 1:
                for mt in range(4):
                    tail_store(b, mt, "s,v,v,s".split(",")[mt])
            else:
                for k in range(4):
                    tail_store2(b, k // 2, k % 2, "s,v,v,s".split(",")[k])
